import numpy as np
import ml_dtypes


def mxq(x, axis, fmt="e4m3"):
    dtype, down = {"e4m3": (ml_dtypes.float8_e4m3fn, 7), "e5m2": (ml_dtypes.float8_e5m2, 14)}[fmt]
    v = np.moveaxis(np.asarray(x, np.float32).astype(ml_dtypes.bfloat16).astype(np.float64), axis, -1)
    blocks = v.reshape(v.shape[:-1] + (-1, 32))
    amax = np.abs(blocks).max(-1, keepdims=True)
    byte = np.maximum(np.where(amax > 0, np.frexp(amax)[1] - 1 + 127, 0) - down, 1)
    scale = np.exp2(byte - 127.0)
    codes = (blocks / scale).astype(np.float32).astype(dtype).astype(np.float64)
    return np.moveaxis((codes * scale).reshape(v.shape), -1, axis)


WIDE = False


def mx_kscale(k):
    if not WIDE:
        return np.ones(k)
    levels = np.array([10, -10, 5, -5, 0])
    a = np.random.permutation(np.resize(levels, k // 512 * 4)).reshape(k // 512, 4)
    idx = np.arange(k)
    return np.exp2(a[idx // 512, idx % 128 // 32])


BF16 = ml_dtypes.bfloat16


def bf(x):
    return np.asarray(x, np.float32).astype(BF16)


def f64(x):
    return np.asarray(x).astype(np.float64)


M, DI, N, DO, TS = 4096, 1024, 512, 1024, 3
DENSITY = 0.25


def setup_inputs():
    k = mx_kscale(N)
    m = (np.random.uniform(size=(N, N)) < DENSITY).astype(np.float64)
    return {'state': bf(np.tanh(1.2 * np.random.standard_normal((M, N))) * k),
            'weights': bf(np.random.standard_normal((N, N)) * 1.5 / np.sqrt(DENSITY * N) / k[:, None]),
            'J': bf(np.random.standard_normal((N, N)) * 2.0 / np.sqrt(DENSITY * N)),
            'theta': bf(np.random.uniform(size=N) * 1.0 + 0.25),
            'lam': bf(0.35 + 0.05 * np.random.standard_normal(1)),
            'mask': bf(m * (1.0 - np.eye(N))),
            'noise_raw': bf(np.random.standard_normal((M, N)) * 2.5),
            'W_out': bf(np.random.standard_normal((DO, N)) * 1.5 / np.sqrt(N)),
            'b_out': bf(np.random.standard_normal(DO) * 0.3)}


def reference(state, weights, J, theta, lam, mask, noise_raw, W_out, b_out):
    st = f64(state)
    eff_w = f64(weights) * f64(mask)
    J_m = f64(J) * f64(mask)
    T = np.abs(np.sin(2.0 * f64(theta)))
    signal = mxq(st, 1, 'e4m3') @ mxq(eff_w, 0, 'e4m3')
    s = np.tanh(st)
    delta = (mxq(s, 1, 'e4m3') @ mxq(J_m, 0, 'e4m3')) * s
    noise = f64(noise_raw) * T * 0.1
    new_state = np.tanh(signal + f64(lam) * delta + noise)
    return (mxq(new_state, 1, 'e4m3') @ mxq(f64(W_out), 1, 'e4m3').T) + f64(b_out)

@@ -1,0 +1,388 @@
+import math
+from contextlib import ExitStack
+
+import concourse.mybir as mybir
+from concourse.masks import make_identity
+
+F32 = mybir.dt.float32
+BF16 = mybir.dt.bfloat16
+I32 = mybir.dt.int32
+U32 = mybir.dt.uint32
+U8 = mybir.dt.uint8
+FP8X4 = mybir.dt.float8_e4m3fn_x4
+ALU = mybir.AluOpType
+ACT = mybir.ActivationFunctionType
+
+P = 128
+TOKENS = 4096
+NEURONS = 512
+OUTS = 1024
+CHUNK = 512
+N_CHUNKS = TOKENS // CHUNK
+GROUPS = 4 * N_CHUNKS
+LAG_OUT = 6
+PI_HI = 3.1415927410125732
+PI_LO = -8.742277657347586e-08
+PINNED = True
+
+FLOPS = 2 * TOKENS * NEURONS * (2 * NEURONS + OUTS)
+
+
+def tile_brainquantumlayer_pc_t_kernel(tc, state, weights, J, theta, lam, mask, noise_raw, W_out, b_out, out):
+    nc = tc.nc
+    with ExitStack() as ctx:
+        if PINNED:
+            ctx.enter_context(tc.manual_schedule())
+        const = ctx.enter_context(tc.tile_pool(name="const", bufs=1))
+        work = ctx.enter_context(tc.tile_pool(name="work", bufs=2))
+        psum = ctx.enter_context(tc.psum_pool(name="psum", bufs=1))
+
+        ident = const.tile([P, P], F32, name="ident")
+        st_all = const.tile([P, N_CHUNKS * 2048], BF16, name="st_all")
+        nz_all = const.tile([P, N_CHUNKS * 2048], BF16, name="nz_all")
+        th_raw = const.tile([P, 4], BF16, name="th_raw")
+        lam_raw = const.tile([P, 1], BF16, name="lam_raw")
+        b_bc = const.tile([P, OUTS], BF16, name="b_bc")
+        w_raw = const.tile([P, 2048], BF16, name="w_raw")
+        m_raw = const.tile([P, 2048], BF16, name="m_raw")
+        j_raw = const.tile([P, 2048], BF16, name="j_raw")
+        wo_raw = const.tile([P, 4096], BF16, name="wo_raw")
+        g_w = const.tile([P, 2048], BF16, name="g_w", align_bytes=64)
+        g_j = const.tile([P, 2048], BF16, name="g_j", align_bytes=64)
+        g_wo = const.tile([P, 4096], BF16, name="g_wo", align_bytes=64)
+        c_w = const.tile([P, 512], U32, name="c_w", align_bytes=64)
+        c_j = const.tile([P, 512], U32, name="c_j", align_bytes=64)
+        c_wo = const.tile([P, 1024], U32, name="c_wo", align_bytes=64)
+        s_w = const.tile([P, 512], U8, name="s_w", align_bytes=64)
+        s_j = const.tile([P, 512], U8, name="s_j", align_bytes=64)
+        s_wo = const.tile([P, 1024], U8, name="s_wo", align_bytes=64)
+        lam_f = const.tile([P, 1], F32, name="lam_f")
+        t01 = const.tile([P, 4], F32, name="t01")
+
+        st_words = st_all[:].bitcast(F32)
+        nz_words = nz_all[:].bitcast(F32)
+
+        def load_rows(dst, src, c):
+            nc.sync.dma_start(
+                out=dst[:, c * 2048 : (c + 1) * 2048],
+                in_=src[c * CHUNK : (c + 1) * CHUNK, :].rearrange("(p j) k -> p (j k)", j=4),
+            )
+
+        def load_k_first(dst, src):
+            nc.sync.dma_start(
+                out=dst[:].rearrange("p (u x) -> p u x", u=2),
+                in_=src.rearrange("(u p e) n -> p u (e n)", u=2, e=2),
+            )
+
+        nc.scalar.dma_start(out=th_raw[:].rearrange("p (u e) -> p u e", u=2), in_=theta.rearrange("(u p e) -> p u e", u=2, e=2))
+        nc.scalar.dma_start(out=lam_raw[:], in_=lam.partition_broadcast(P))
+        make_identity(nc, ident[:])
+        load_rows(st_all, state, 0)
+        load_k_first(m_raw, mask)
+        load_k_first(j_raw, J)
+        load_k_first(w_raw, weights)
+        load_rows(nz_all, noise_raw, 0)
+        load_rows(st_all, state, 1)
+        nc.sync.dma_start(out=wo_raw[:].rearrange("p (r k) -> p r k", r=8), in_=W_out.rearrange("(r p) k -> p r k", p=P))
+        load_rows(nz_all, noise_raw, 1)
+        load_rows(st_all, state, 2)
+        nc.sync.dma_start(out=b_bc[:], in_=b_out.partition_broadcast(P))
+        load_rows(nz_all, noise_raw, 2)
+        for c in range(3, N_CHUNKS):
+            load_rows(st_all, state, c)
+            load_rows(nz_all, noise_raw, c)
+
+        x2 = const.tile([P, 4], F32, name="x2")
+        yy = const.tile([P, 4], F32, name="yy")
+        ki = const.tile([P, 4], I32, name="ki")
+        kf = const.tile([P, 4], F32, name="kf")
+        r1 = const.tile([P, 4], F32, name="r1")
+        r2 = const.tile([P, 4], F32, name="r2")
+        sn = const.tile([P, 4], F32, name="sn")
+        nc.vector.tensor_scalar(out=yy[:], in0=th_raw[:], scalar1=2.0 / math.pi, scalar2=None, op0=ALU.mult)
+        nc.vector.tensor_scalar(out=x2[:], in0=th_raw[:], scalar1=2.0, scalar2=None, op0=ALU.mult)
+        nc.vector.tensor_copy(out=ki[:], in_=yy[:])
+        nc.vector.tensor_copy(out=kf[:], in_=ki[:])
+        nc.vector.scalar_tensor_tensor(out=r1[:], in0=kf[:], scalar=-PI_HI, in1=x2[:], op0=ALU.mult, op1=ALU.add)
+        nc.vector.scalar_tensor_tensor(out=r2[:], in0=kf[:], scalar=-PI_LO, in1=r1[:], op0=ALU.mult, op1=ALU.add)
+        nc.scalar.activation(out=sn[:], in_=r2[:], func=ACT.Sin)
+        nc.scalar.activation(out=t01[:], in_=sn[:], func=ACT.Abs, scale=0.1)
+        nc.vector.tensor_copy(out=lam_f[:], in_=lam_raw[:])
+
+        def masked_weights(raw, grouped, u):
+            nc.vector.tensor_tensor(
+                out=grouped[:, u * 1024 : (u + 1) * 1024].rearrange("p (e q t) -> p e q t", e=2, t=4),
+                in0=raw[:].rearrange("p (t u q e) -> p u e q t", t=4, u=2, e=2)[:, u],
+                in1=m_raw[:].rearrange("p (t u q e) -> p u e q t", t=4, u=2, e=2)[:, u],
+                op=ALU.mult,
+            )
+
+        tiles = {}
+
+        def transpose_state(c, h):
+            ts = psum.tile([P, 512], F32, name="ts%d" % h)
+            tiles[("ts", c, h)] = ts
+            for jj in range(2):
+                for u in range(2):
+                    col = c * 1024 + (2 * h + jj) * 256 + u * 128
+                    nc.tensor.transpose(out=ts[:, u * 256 + jj * 128 : u * 256 + (jj + 1) * 128], in_=st_words[:, col : col + 128], identity=ident[:])
+
+        def copy_state(c, h):
+            if h == 0:
+                tiles[("gst", c)] = work.tile([P, 2048], BF16, name="gst", align_bytes=64)
+            ts = tiles[("ts", c, h)]
+            nc.scalar.copy(
+                out=tiles[("gst", c)][:].bitcast(F32)[:, h * 512 : (h + 1) * 512].rearrange("p (m u) -> p m u", u=2),
+                in_=ts[:].rearrange("p (u m) -> p m u", u=2),
+            )
+
+        def tanh_state_bf16(c, h):
+            if h == 0:
+                tiles[("gs", c)] = work.tile([P, 2048], BF16, name="gs", align_bytes=64)
+            ts = tiles[("ts", c, h)]
+            nc.scalar.activation(
+                out=tiles[("gs", c)][:, h * 1024 : (h + 1) * 1024].rearrange("p (m u e) -> p m u e", u=2, e=2),
+                in_=ts[:].bitcast(BF16).rearrange("p (u m e) -> p m u e", u=2, e=2),
+                func=ACT.Tanh,
+            )
+
+        def tanh_state_f32(c, h):
+            if h == 0:
+                tiles[("sf", c)] = work.tile([P, 2048], F32, name="sf")
+            ts = tiles[("ts", c, h)]
+            nc.scalar.activation(
+                out=tiles[("sf", c)][:].rearrange("p (u e x) -> p u e x", u=2, e=2)[:, :, :, h * 256 : (h + 1) * 256],
+                in_=ts[:].bitcast(BF16).rearrange("p (u m e) -> p u e m", u=2, e=2),
+                func=ACT.Tanh,
+            )
+
+        def quantise(key, c, bufs):
+            codes = work.tile([P, 512], U32, name="c" + key, bufs=bufs, align_bytes=64)
+            scales = work.tile([P, 512], U8, name="s" + key, bufs=bufs, align_bytes=64)
+            tiles[("c" + key, c)] = codes
+            tiles[("s" + key, c)] = scales
+            nc.vector.quantize_mx(out=codes[:].bitcast(FP8X4), scales=scales[:], in_=tiles[("g" + key, c)][:])
+
+        def transpose_noise(c, u):
+            tn = psum.tile([P, 512], F32, name="tn%d" % u)
+            tiles[("tn", c, u)] = tn
+            for j in range(4):
+                col = c * 1024 + j * 256 + u * 128
+                nc.tensor.transpose(out=tn[:, j * 128 : (j + 1) * 128], in_=nz_words[:, col : col + 128], identity=ident[:])
+
+        def stage1(kind, c, t):
+            acc = psum.tile([P, 512], F32, name="p" + kind)
+            tiles[("p" + kind, c, t)] = acc
+            cw, sw, key = (c_j, s_j, "s") if kind == "d" else (c_w, s_w, "st")
+            nc.tensor.matmul_mx(
+                out=acc[:],
+                lhsT=cw[:, t * P : (t + 1) * P].bitcast(FP8X4),
+                lhsT_scale=sw[:, t * P : (t + 1) * P],
+                rhs=tiles[("c" + key, c)][:].bitcast(FP8X4),
+                rhs_scale=tiles[("s" + key, c)][:],
+                start=True,
+                stop=True,
+            )
+
+        def delta_times_s(c, t):
+            d = work.tile([P, 512], F32, name="d")
+            tiles[("d", c, t)] = d
+            nc.vector.scalar_tensor_tensor(
+                out=d[:], in0=tiles[("pd", c, t)][:], scalar=lam_f[:, 0:1], in1=tiles[("sf", c)][:, t * 512 : (t + 1) * 512], op0=ALU.mult, op1=ALU.mult
+            )
+
+        def add_noise(c, t):
+            e = work.tile([P, 512], F32, name="e")
+            tiles[("e", c, t)] = e
+            nc.vector.scalar_tensor_tensor(
+                out=e[:],
+                in0=tiles[("tn", c, t // 2)][:].bitcast(BF16).rearrange("p (m e) -> p e m", e=2)[:, t % 2, :],
+                scalar=t01[:, t : t + 1],
+                in1=tiles[("d", c, t)][:],
+                op0=ALU.mult,
+                op1=ALU.add,
+            )
+
+        def add_signal(c, t):
+            if t == 0:
+                tiles[("f", c)] = work.tile([P, 2048], F32, name="f")
+            nc.vector.tensor_tensor(out=tiles[("f", c)][:, t * 512 : (t + 1) * 512], in0=tiles[("ps", c, t)][:], in1=tiles[("e", c, t)][:], op=ALU.add)
+
+        def tanh_new_state(c, lo, n):
+            if lo == 0:
+                tiles[("gns", c)] = work.tile([P, 2048], BF16, name="gns", align_bytes=64)
+            nc.scalar.activation(
+                out=tiles[("gns", c)][:, lo * 4 : (lo + n) * 4].rearrange("p (m t) -> p m t", t=4),
+                in_=tiles[("f", c)][:].rearrange("p (t m) -> p m t", t=4)[:, lo : lo + n, :],
+                func=ACT.Tanh,
+            )
+
+        def quantise_new_state(c, lo, n):
+            if lo == 0:
+                tiles[("cns", c)] = work.tile([P, 512], U32, name="cns", align_bytes=64)
+                tiles[("sns", c)] = work.tile([P, 512], U8, name="sns", align_bytes=64)
+            nc.vector.quantize_mx(
+                out=tiles[("cns", c)][:, lo : lo + n].bitcast(FP8X4),
+                scales=tiles[("sns", c)][:, lo : lo + n],
+                in_=tiles[("gns", c)][:, lo * 4 : (lo + n) * 4],
+            )
+
+        def stage2(c, j, o, tag):
+            acc = psum.tile([P, 512], F32, name=tag)
+            tiles[("po", c, j, o)] = acc
+            nc.tensor.matmul_mx(
+                out=acc[:],
+                lhsT=tiles[("cns", c)][:, j * P : (j + 1) * P].bitcast(FP8X4),
+                lhsT_scale=tiles[("sns", c)][:, j * P : (j + 1) * P],
+                rhs=c_wo[:, o * 512 : (o + 1) * 512].bitcast(FP8X4),
+                rhs_scale=s_wo[:, o * 512 : (o + 1) * 512],
+                start=True,
+                stop=True,
+            )
+
+        def out_tile(c, j):
+            if ("ot", c, j) not in tiles:
+                tiles[("ot", c, j)] = work.tile([P, OUTS], F32, name="ot", bufs=6)
+            return tiles[("ot", c, j)]
+
+        def out_vector(c, j, o):
+            cols = slice(o * 512, (o + 1) * 512)
+            nc.vector.tensor_tensor(out=out_tile(c, j)[:, cols], in0=tiles[("po", c, j, o)][:], in1=b_bc[:, cols], op=ALU.add)
+
+        def out_scalar(c, j, o):
+            cols = slice(o * 512, (o + 1) * 512)
+            ot = out_tile(c, j)
+            nc.scalar.copy(out=ot[:, cols], in_=tiles[("po", c, j, o)][:])
+            nc.gpsimd.tensor_tensor(out=ot[:, cols], in0=ot[:, cols], in1=b_bc[:, cols], op=ALU.add)
+
+        def store(c, j):
+            nc.sync.dma_start(out=out[c * CHUNK : (c + 1) * CHUNK, :].rearrange("(p j) o -> p j o", j=4)[:, j, :], in_=tiles[("ot", c, j)][:])
+
+        def transpose_w_out(b):
+            pw = psum.tile([P, 512], F32, name=("ov", "os")[b % 2])
+            tiles[("pw", b)] = pw
+            for rr in range(2):
+                for u in range(2):
+                    col = (2 * b + rr) * 256 + u * 128
+                    nc.tensor.transpose(out=pw[:, u * 256 + rr * 128 : u * 256 + (rr + 1) * 128], in_=wo_raw[:].bitcast(F32)[:, col : col + 128], identity=ident[:])
+
+        def copy_w_out(b):
+            nc.scalar.copy(
+                out=g_wo[:].bitcast(F32)[:, b * 512 : (b + 1) * 512].rearrange("p (m u) -> p m u", u=2),
+                in_=tiles[("pw", b)][:].rearrange("p (u m) -> p m u", u=2),
+            )
+
+        def ok(c):
+            return 0 <= c < N_CHUNKS
+
+        masked_weights(j_raw, g_j, 0)
+        masked_weights(j_raw, g_j, 1)
+        nc.vector.quantize_mx(out=c_j[:].bitcast(FP8X4), scales=s_j[:], in_=g_j[:])
+        transpose_state(0, 0)
+        transpose_state(0, 1)
+        tanh_state_bf16(0, 0)
+        tanh_state_bf16(0, 1)
+        tanh_state_f32(0, 0)
+        tanh_state_f32(0, 1)
+        copy_state(0, 0)
+        copy_state(0, 1)
+        quantise("s", 0, 2)
+        stage1("d", 0, 0)
+        masked_weights(w_raw, g_w, 0)
+        masked_weights(w_raw, g_w, 1)
+        nc.vector.quantize_mx(out=c_w[:].bitcast(FP8X4), scales=s_w[:], in_=g_w[:])
+        quantise("st", 0, 2)
+        transpose_noise(0, 0)
+        transpose_noise(0, 1)
+        transpose_state(1, 0)
+        transpose_state(1, 1)
+        copy_state(1, 0)
+        copy_state(1, 1)
+        tanh_state_bf16(1, 0)
+        tanh_state_bf16(1, 1)
+
+        for q in range(0, GROUPS):
+            i, g = q // 4, q % 4
+            qo = q - LAG_OUT
+            co, jo = qo // 4, qo % 4
+            a = i + 2 if g > 0 else i + 1
+            if g == 0 and ok(a):
+                tanh_state_f32(a, 0)
+                tanh_state_f32(a, 1)
+            if g == 1 and ok(i - 1):
+                tanh_new_state(i - 1, 0, 256)
+            if g == 2 and ok(i - 1):
+                tanh_new_state(i - 1, 256, 256)
+            if g == 3 and ok(a):
+                tanh_state_bf16(a, 0)
+            if g == 1 and ok(i + 1):
+                quantise("st", i + 1, 2)
+            if g == 2 and ok(i - 1):
+                quantise_new_state(i - 1, 0, 256)
+            if g == 2 and ok(i + 1):
+                quantise("s", i + 1, 2)
+            if g == 3 and ok(i - 1):
+                quantise_new_state(i - 1, 256, 256)
+            if q == 5:
+                nc.vector.quantize_mx(out=c_wo[:].bitcast(FP8X4), scales=s_wo[:], in_=g_wo[:])
+            if ok(co):
+                stage2(co, jo, 0, "ov")
+                stage2(co, jo, 1, "os")
+            delta_times_s(i, g)
+            if ok((q + 1) // 4):
+                stage1("d", (q + 1) // 4, (q + 1) % 4)
+            if ok((q - 1) // 4):
+                add_signal((q - 1) // 4, (q - 1) % 4)
+            stage1("s", i, g)
+            add_noise(i, g)
+            if ok(co):
+                out_vector(co, jo, 0)
+                out_scalar(co, jo, 1)
+                store(co, jo)
+            if 0 <= q < 4:
+                transpose_w_out(q)
+                copy_w_out(q)
+            if g == 0:
+                if ok(a + 1):
+                    transpose_state(a + 1, 0)
+                    transpose_state(a + 1, 1)
+                if i > 0:
+                    transpose_noise(i, 1)
+            if g == 1 and ok(a):
+                copy_state(a, 0)
+            if g == 2:
+                if ok(i + 1):
+                    transpose_noise(i + 1, 0)
+                if ok(a):
+                    copy_state(a, 1)
+            if g == 3 and ok(a):
+                tanh_state_bf16(a, 1)
+
+        last = N_CHUNKS - 1
+        add_signal(last, 3)
+        for j in range(4):
+            tanh_new_state(last, j * P, P)
+        stage2(last - 1, 2, 0, "ov")
+        stage2(last - 1, 2, 1, "os")
+        stage2(last - 1, 3, 0, "pd")
+        stage2(last - 1, 3, 1, "ps")
+        out_vector(last - 1, 2, 0)
+        out_vector(last - 1, 2, 1)
+        store(last - 1, 2)
+        quantise_new_state(last, 0, P)
+        out_vector(last - 1, 3, 0)
+        quantise_new_state(last, P, P)
+        out_vector(last - 1, 3, 1)
+        store(last - 1, 3)
+        quantise_new_state(last, 2 * P, P)
+        quantise_new_state(last, 3 * P, P)
+        for j, tags in enumerate((("tn0", "tn1"), ("ts0", "ts1"), ("ov", "os"), ("pd", "ps"))):
+            stage2(last, j, 0, tags[0])
+            stage2(last, j, 1, tags[1])
+        for j in range(4):
+            out_vector(last, j, 0)
+            if j < 2:
+                out_scalar(last, j, 1)
+            else:
+                out_vector(last, j, 1)
+            store(last, j)

@@ -219,8 +219,8 @@ def tile_brainquantumlayer_pc_t_kernel(tc, state, weights, J, theta, lam, mask, 
 
         def quantise_new_state(c, lo, n):
             if lo == 0:
-                tiles[("cns", c)] = work.tile([P, 512], U32, name="cns", align_bytes=64)
-                tiles[("sns", c)] = work.tile([P, 512], U8, name="sns", align_bytes=64)
+                tiles[("cns", c)] = work.tile([P, 512], U32, name="cns", bufs=3, align_bytes=64)
+                tiles[("sns", c)] = work.tile([P, 512], U8, name="sns", bufs=3, align_bytes=64)
             nc.vector.quantize_mx(
                 out=tiles[("cns", c)][:, lo : lo + n].bitcast(FP8X4),
                 scales=tiles[("sns", c)][:, lo : lo + n],
@@ -242,7 +242,7 @@ def tile_brainquantumlayer_pc_t_kernel(tc, state, weights, J, theta, lam, mask, 
 
         def out_tile(c, j):
             if ("ot", c, j) not in tiles:
-                tiles[("ot", c, j)] = work.tile([P, OUTS], F32, name="ot", bufs=6)
+                tiles[("ot", c, j)] = work.tile([P, OUTS], F32, name="ot", bufs=8)
             return tiles[("ot", c, j)]
 
         def out_vector(c, j, o):
@@ -267,7 +267,7 @@ def tile_brainquantumlayer_pc_t_kernel(tc, state, weights, J, theta, lam, mask, 
                     nc.tensor.transpose(out=pw[:, u * 256 + rr * 128 : u * 256 + (rr + 1) * 128], in_=wo_raw[:].bitcast(F32)[:, col : col + 128], identity=ident[:])
 
         def copy_w_out(b):
-            nc.scalar.copy(
+            nc.vector.tensor_copy(
                 out=g_wo[:].bitcast(F32)[:, b * 512 : (b + 1) * 512].rearrange("p (m u) -> p m u", u=2),
                 in_=tiles[("pw", b)][:].rearrange("p (u m) -> p m u", u=2),
             )
@@ -301,88 +301,92 @@ def tile_brainquantumlayer_pc_t_kernel(tc, state, weights, J, theta, lam, mask, 
         tanh_state_bf16(1, 0)
         tanh_state_bf16(1, 1)
 
-        for q in range(0, GROUPS):
-            i, g = q // 4, q % 4
-            qo = q - LAG_OUT
-            co, jo = qo // 4, qo % 4
-            a = i + 2 if g > 0 else i + 1
-            if g == 0 and ok(a):
-                tanh_state_f32(a, 0)
-                tanh_state_f32(a, 1)
-            if g == 1 and ok(i - 1):
-                tanh_new_state(i - 1, 0, 256)
-            if g == 2 and ok(i - 1):
-                tanh_new_state(i - 1, 256, 256)
-            if g == 3 and ok(a):
-                tanh_state_bf16(a, 0)
-            if g == 1 and ok(i + 1):
+        for i in range(N_CHUNKS):
+            co = i - 2
+            if i == 1:
+                copy_w_out(3)
+            if ok(co):
+                quantise_new_state(co, 0, CHUNK)
+            if i > 0 and ok(i + 1):
                 quantise("st", i + 1, 2)
-            if g == 2 and ok(i - 1):
-                quantise_new_state(i - 1, 0, 256)
-            if g == 2 and ok(i + 1):
                 quantise("s", i + 1, 2)
-            if g == 3 and ok(i - 1):
-                quantise_new_state(i - 1, 256, 256)
-            if q == 5:
+            if i == 2:
                 nc.vector.quantize_mx(out=c_wo[:].bitcast(FP8X4), scales=s_wo[:], in_=g_wo[:])
+            if ok(i + 1):
+                tanh_state_f32(i + 1, 0)
+                tanh_state_f32(i + 1, 1)
             if ok(co):
-                stage2(co, jo, 0, "ov")
-                stage2(co, jo, 1, "os")
-            delta_times_s(i, g)
-            if ok((q + 1) // 4):
-                stage1("d", (q + 1) // 4, (q + 1) % 4)
-            if ok((q - 1) // 4):
-                add_signal((q - 1) // 4, (q - 1) % 4)
-            stage1("s", i, g)
-            add_noise(i, g)
-            if ok(co):
-                out_vector(co, jo, 0)
-                out_scalar(co, jo, 1)
-                store(co, jo)
-            if 0 <= q < 4:
-                transpose_w_out(q)
-                copy_w_out(q)
-            if g == 0:
-                if ok(a + 1):
-                    transpose_state(a + 1, 0)
-                    transpose_state(a + 1, 1)
-                if i > 0:
-                    transpose_noise(i, 1)
-            if g == 1 and ok(a):
-                copy_state(a, 0)
-            if g == 2:
-                if ok(i + 1):
-                    transpose_noise(i + 1, 0)
-                if ok(a):
-                    copy_state(a, 1)
-            if g == 3 and ok(a):
-                tanh_state_bf16(a, 1)
+                stage2(co, 0, 0, "ov")
+                stage2(co, 0, 1, "os")
+            if i > 0:
+                transpose_noise(i, 1)
+            if i > 0 and ok(i + 2):
+                transpose_state(i + 2, 0)
+                transpose_state(i + 2, 1)
+                copy_state(i + 2, 0)
+            for g in range(4):
+                q = 4 * i + g
+                delta_times_s(i, g)
+                if ok((q + 1) // 4):
+                    stage1("d", (q + 1) // 4, (q + 1) % 4)
+                if q > 0:
+                    add_signal((q - 1) // 4, (q - 1) % 4)
+                stage1("s", i, g)
+                add_noise(i, g)
+                if ok(co):
+                    out_scalar(co, g, 1)
+                    out_vector(co, g, 0)
+                    store(co, g)
+                    if g < 3:
+                        stage2(co, g + 1, 1, "os")
+                        stage2(co, g + 1, 0, "ov")
+                if i == 0:
+                    if g > 0:
+                        copy_w_out(g - 1)
+                    transpose_w_out(g)
+                    if g == 2:
+                        quantise("st", 1, 2)
+                        quantise("s", 1, 2)
+                if g == 0 and ok(i - 1):
+                    tanh_new_state(i - 1, 0, 256)
+                if g == 1:
+                    if ok(i - 1):
+                        tanh_new_state(i - 1, 256, 256)
+                    if ok(i + 1):
+                        transpose_noise(i + 1, 0)
+                if g == 1 and i == 0:
+                    transpose_state(2, 0)
+                    transpose_state(2, 1)
+                    copy_state(2, 0)
+                if g == 2 and ok(i + 2):
+                    copy_state(i + 2, 1)
+                if g == 3 and ok(i + 2):
+                    tanh_state_bf16(i + 2, 0)
+                    tanh_state_bf16(i + 2, 1)
 
         last = N_CHUNKS - 1
+        quantise_new_state(last - 1, 0, CHUNK)
         add_signal(last, 3)
         for j in range(4):
             tanh_new_state(last, j * P, P)
-        stage2(last - 1, 2, 0, "ov")
-        stage2(last - 1, 2, 1, "os")
-        stage2(last - 1, 3, 0, "pd")
-        stage2(last - 1, 3, 1, "ps")
-        out_vector(last - 1, 2, 0)
-        out_vector(last - 1, 2, 1)
-        store(last - 1, 2)
-        quantise_new_state(last, 0, P)
-        out_vector(last - 1, 3, 0)
-        quantise_new_state(last, P, P)
-        out_vector(last - 1, 3, 1)
-        store(last - 1, 3)
-        quantise_new_state(last, 2 * P, P)
-        quantise_new_state(last, 3 * P, P)
-        for j, tags in enumerate((("tn0", "tn1"), ("ts0", "ts1"), ("ov", "os"), ("pd", "ps"))):
-            stage2(last, j, 0, tags[0])
-            stage2(last, j, 1, tags[1])
+        banks = ("ov", "os", "pd", "ps", "tn0", "tn1", "ts0", "ts1")
         for j in range(4):
-            out_vector(last, j, 0)
-            if j < 2:
+            stage2(last - 1, j, 0, banks[2 * j])
+            stage2(last - 1, j, 1, banks[2 * j + 1])
+        for j in range(4):
+            out_vector(last - 1, j, 0)
+            if j < 3:
+                out_vector(last - 1, j, 1)
+            else:
+                out_scalar(last - 1, j, 1)
+            store(last - 1, j)
+            quantise_new_state(last, j * P, P)
+            stage2(last, j, 1, banks[2 * j + 1])
+            stage2(last, j, 0, banks[2 * j])
+        for j in range(4):
+            if j < 3:
                 out_scalar(last, j, 1)
             else:
                 out_vector(last, j, 1)
+            out_vector(last, j, 0)
             store(last, j)

@@ -24,6 +24,8 @@ LAG_OUT = 6
 PI_HI = 3.1415927410125732
 PI_LO = -8.742277657347586e-08
 PINNED = True
+W_OUT_ON_SCALAR = 2
+LATE = 8
 
 FLOPS = 2 * TOKENS * NEURONS * (2 * NEURONS + OUTS)
 
@@ -109,8 +111,8 @@ def tile_brainquantumlayer_pc_t_kernel(tc, state, weights, J, theta, lam, mask, 
         nc.scalar.activation(out=t01[:], in_=sn[:], func=ACT.Abs, scale=0.1)
         nc.vector.tensor_copy(out=lam_f[:], in_=lam_raw[:])
 
-        def masked_weights(raw, grouped, u):
-            nc.vector.tensor_tensor(
+        def masked_weights(eng, raw, grouped, u):
+            eng.tensor_tensor(
                 out=grouped[:, u * 1024 : (u + 1) * 1024].rearrange("p (e q t) -> p e q t", e=2, t=4),
                 in0=raw[:].rearrange("p (t u q e) -> p u e q t", t=4, u=2, e=2)[:, u],
                 in1=m_raw[:].rearrange("p (t u q e) -> p u e q t", t=4, u=2, e=2)[:, u],
@@ -267,7 +269,8 @@ def tile_brainquantumlayer_pc_t_kernel(tc, state, weights, J, theta, lam, mask, 
                     nc.tensor.transpose(out=pw[:, u * 256 + rr * 128 : u * 256 + (rr + 1) * 128], in_=wo_raw[:].bitcast(F32)[:, col : col + 128], identity=ident[:])
 
         def copy_w_out(b):
-            nc.vector.tensor_copy(
+            copier = nc.scalar.copy if b < W_OUT_ON_SCALAR else nc.vector.tensor_copy
+            copier(
                 out=g_wo[:].bitcast(F32)[:, b * 512 : (b + 1) * 512].rearrange("p (m u) -> p m u", u=2),
                 in_=tiles[("pw", b)][:].rearrange("p (u m) -> p m u", u=2),
             )
@@ -275,8 +278,8 @@ def tile_brainquantumlayer_pc_t_kernel(tc, state, weights, J, theta, lam, mask, 
         def ok(c):
             return 0 <= c < N_CHUNKS
 
-        masked_weights(j_raw, g_j, 0)
-        masked_weights(j_raw, g_j, 1)
+        masked_weights(nc.vector, j_raw, g_j, 0)
+        masked_weights(nc.vector, j_raw, g_j, 1)
         nc.vector.quantize_mx(out=c_j[:].bitcast(FP8X4), scales=s_j[:], in_=g_j[:])
         transpose_state(0, 0)
         transpose_state(0, 1)
@@ -288,10 +291,8 @@ def tile_brainquantumlayer_pc_t_kernel(tc, state, weights, J, theta, lam, mask, 
         copy_state(0, 1)
         quantise("s", 0, 2)
         stage1("d", 0, 0)
-        masked_weights(w_raw, g_w, 0)
-        masked_weights(w_raw, g_w, 1)
-        nc.vector.quantize_mx(out=c_w[:].bitcast(FP8X4), scales=s_w[:], in_=g_w[:])
-        quantise("st", 0, 2)
+        masked_weights(nc.vector, w_raw, g_w, 0)
+        masked_weights(nc.vector, w_raw, g_w, 1)
         transpose_noise(0, 0)
         transpose_noise(0, 1)
         transpose_state(1, 0)
@@ -303,27 +304,24 @@ def tile_brainquantumlayer_pc_t_kernel(tc, state, weights, J, theta, lam, mask, 
 
         for i in range(N_CHUNKS):
             co = i - 2
-            if i == 1:
+            if i == 2:
                 copy_w_out(3)
             if ok(co):
                 quantise_new_state(co, 0, CHUNK)
             if i > 0 and ok(i + 1):
                 quantise("st", i + 1, 2)
-                quantise("s", i + 1, 2)
             if i == 2:
                 nc.vector.quantize_mx(out=c_wo[:].bitcast(FP8X4), scales=s_wo[:], in_=g_wo[:])
+            if i > 0 and ok(i + 1):
+                quantise("s", i + 1, 2)
             if ok(i + 1):
                 tanh_state_f32(i + 1, 0)
                 tanh_state_f32(i + 1, 1)
             if ok(co):
-                stage2(co, 0, 0, "ov")
                 stage2(co, 0, 1, "os")
-            if i > 0:
-                transpose_noise(i, 1)
-            if i > 0 and ok(i + 2):
-                transpose_state(i + 2, 0)
-                transpose_state(i + 2, 1)
-                copy_state(i + 2, 0)
+                stage2(co, 1, 1, "ov")
+                out_scalar(co, 0, 1)
+                out_scalar(co, 1, 1)
             for g in range(4):
                 q = 4 * i + g
                 delta_times_s(i, g)
@@ -331,60 +329,95 @@ def tile_brainquantumlayer_pc_t_kernel(tc, state, weights, J, theta, lam, mask, 
                     stage1("d", (q + 1) // 4, (q + 1) % 4)
                 if q > 0:
                     add_signal((q - 1) // 4, (q - 1) % 4)
+                else:
+                    nc.vector.quantize_mx(out=c_w[:].bitcast(FP8X4), scales=s_w[:], in_=g_w[:])
+                    quantise("st", 0, 2)
                 stage1("s", i, g)
                 add_noise(i, g)
-                if ok(co):
-                    out_scalar(co, g, 1)
-                    out_vector(co, g, 0)
-                    store(co, g)
-                    if g < 3:
-                        stage2(co, g + 1, 1, "os")
-                        stage2(co, g + 1, 0, "ov")
-                if i == 0:
+                if i == 0 and g == 2:
+                    quantise("st", 1, 2)
+                    quantise("s", 1, 2)
+                if i == 1:
                     if g > 0:
                         copy_w_out(g - 1)
                     transpose_w_out(g)
-                    if g == 2:
-                        quantise("st", 1, 2)
-                        quantise("s", 1, 2)
-                if g == 0 and ok(i - 1):
-                    tanh_new_state(i - 1, 0, 256)
+                if g == 0:
+                    if ok(i - 1):
+                        tanh_new_state(i - 1, 0, 256)
+                    if ok(co):
+                        stage2(co, 2, 1, "os")
+                        stage2(co, 0, 0, "ov")
+                        out_scalar(co, 2, 1)
+                    if i > 0 and ok(i + 2):
+                        transpose_state(i + 2, 0)
+                        transpose_state(i + 2, 1)
+                        copy_state(i + 2, 0)
+                    if i > 0:
+                        transpose_noise(i, 1)
                 if g == 1:
                     if ok(i - 1):
                         tanh_new_state(i - 1, 256, 256)
+                    if ok(co):
+                        out_vector(co, 0, 0)
+                        store(co, 0)
+                        stage2(co, 3, 1, "os")
+                        stage2(co, 1, 0, "ov")
+                        out_scalar(co, 3, 1)
                     if ok(i + 1):
                         transpose_noise(i + 1, 0)
-                if g == 1 and i == 0:
-                    transpose_state(2, 0)
-                    transpose_state(2, 1)
-                    copy_state(2, 0)
-                if g == 2 and ok(i + 2):
-                    copy_state(i + 2, 1)
-                if g == 3 and ok(i + 2):
-                    tanh_state_bf16(i + 2, 0)
-                    tanh_state_bf16(i + 2, 1)
+                    if i == 0:
+                        transpose_state(2, 0)
+                        transpose_state(2, 1)
+                        copy_state(2, 0)
+                if g == 2:
+                    if ok(co):
+                        out_vector(co, 1, 0)
+                        store(co, 1)
+                        stage2(co, 3, 0, "os")
+                        stage2(co, 2, 0, "ov")
+                    if ok(i + 2):
+                        copy_state(i + 2, 1)
+                if g == 3:
+                    if i == N_CHUNKS - 1:
+                        quantise_new_state(i - 1, 0, CHUNK)
+                        stage2(i - 1, 0, 1, "ts0")
+                        stage2(i - 1, 1, 1, "ts1")
+                    if ok(co):
+                        if i >= LATE:
+                            out_scalar(co, 2, 0)
+                        else:
+                            out_vector(co, 2, 0)
+                        store(co, 2)
+                        out_vector(co, 3, 0)
+                        store(co, 3)
+                    if ok(i + 2):
+                        tanh_state_bf16(i + 2, 0)
+                        tanh_state_bf16(i + 2, 1)
 
         last = N_CHUNKS - 1
-        quantise_new_state(last - 1, 0, CHUNK)
+        out_scalar(last - 1, 0, 1)
+        out_scalar(last - 1, 1, 1)
         add_signal(last, 3)
         for j in range(4):
             tanh_new_state(last, j * P, P)
-        banks = ("ov", "os", "pd", "ps", "tn0", "tn1", "ts0", "ts1")
+        for j, o, bank in ((0, 0, "ov"), (1, 0, "os"), (2, 0, "pd"), (2, 1, "ps"), (3, 0, "tn0"), (3, 1, "tn1")):
+            stage2(last - 1, j, o, bank)
+        out_vector(last - 1, 0, 0)
+        store(last - 1, 0)
+        out_vector(last - 1, 1, 0)
+        store(last - 1, 1)
+        out_vector(last - 1, 2, 0)
+        out_vector(last - 1, 2, 1)
+        store(last - 1, 2)
+        quantise_new_state(last, 0, 256)
+        out_vector(last - 1, 3, 0)
+        out_vector(last - 1, 3, 1)
+        store(last - 1, 3)
+        quantise_new_state(last, 256, 256)
+        for j, o, bank in ((0, 1, "ts0"), (0, 0, "ts1"), (1, 1, "ov"), (1, 0, "os"), (2, 0, "pd"), (2, 1, "ps"), (3, 0, "tn0"), (3, 1, "tn1")):
+            stage2(last, j, o, bank)
         for j in range(4):
-            stage2(last - 1, j, 0, banks[2 * j])
-            stage2(last - 1, j, 1, banks[2 * j + 1])
-        for j in range(4):
-            out_vector(last - 1, j, 0)
-            if j < 3:
-                out_vector(last - 1, j, 1)
-            else:
-                out_scalar(last - 1, j, 1)
-            store(last - 1, j)
-            quantise_new_state(last, j * P, P)
-            stage2(last, j, 1, banks[2 * j + 1])
-            stage2(last, j, 0, banks[2 * j])
-        for j in range(4):
-            if j < 3:
+            if j < 2:
                 out_scalar(last, j, 1)
             else:
                 out_vector(last, j, 1)

@@ -150,12 +150,24 @@ def tile_brainquantumlayer_pc_t_kernel(tc, state, weights, J, theta, lam, mask, 
 
         def tanh_state_f32(c, h):
             if h == 0:
-                tiles[("sf", c)] = work.tile([P, 2048], F32, name="sf")
+                tiles[("sf", c)] = work.tile([P, 2048], F32, name="sf", bufs=3)
             ts = tiles[("ts", c, h)]
             nc.scalar.activation(
                 out=tiles[("sf", c)][:].rearrange("p (u e x) -> p u e x", u=2, e=2)[:, :, :, h * 256 : (h + 1) * 256],
                 in_=ts[:].bitcast(BF16).rearrange("p (u m e) -> p u e m", u=2, e=2),
                 func=ACT.Tanh,
+            )
+
+        def round_s(c, h):
+            if h == 0:
+                tiles[("gs", c)] = work.tile([P, 2048], BF16, name="gs", align_bytes=64)
+            nc.gpsimd.tensor_scalar(
+                out=tiles[("gs", c)][:, h * 1024 : (h + 1) * 1024].rearrange("p (m t) -> p m t", t=4),
+                in0=tiles[("sf", c)][:].rearrange("p (t m) -> p m t", t=4)[:, h * 256 : (h + 1) * 256, :],
+                scalar1=1.0,
+                scalar2=0.0,
+                op0=ALU.mult,
+                op1=ALU.add,
             )
 
         def quantise(key, c, bufs):
@@ -244,7 +256,7 @@ def tile_brainquantumlayer_pc_t_kernel(tc, state, weights, J, theta, lam, mask, 
 
         def out_tile(c, j):
             if ("ot", c, j) not in tiles:
-                tiles[("ot", c, j)] = work.tile([P, OUTS], F32, name="ot", bufs=8)
+                tiles[("ot", c, j)] = work.tile([P, OUTS], F32, name="ot", bufs=6)
             return tiles[("ot", c, j)]
 
         def out_vector(c, j, o):
@@ -314,9 +326,14 @@ def tile_brainquantumlayer_pc_t_kernel(tc, state, weights, J, theta, lam, mask, 
                 nc.vector.quantize_mx(out=c_wo[:].bitcast(FP8X4), scales=s_wo[:], in_=g_wo[:])
             if i > 0 and ok(i + 1):
                 quantise("s", i + 1, 2)
-            if ok(i + 1):
-                tanh_state_f32(i + 1, 0)
-                tanh_state_f32(i + 1, 1)
+            if i == 0:
+                tanh_state_f32(1, 0)
+                tanh_state_f32(1, 1)
+            if i > 0 and ok(i + 2):
+                tanh_state_f32(i + 2, 0)
+                round_s(i + 2, 0)
+                tanh_state_f32(i + 2, 1)
+                round_s(i + 2, 1)
             if ok(co):
                 stage2(co, 0, 1, "os")
                 stage2(co, 1, 1, "ov")
@@ -334,7 +351,7 @@ def tile_brainquantumlayer_pc_t_kernel(tc, state, weights, J, theta, lam, mask, 
                     quantise("st", 0, 2)
                 stage1("s", i, g)
                 add_noise(i, g)
-                if i == 0 and g == 2:
+                if i == 0 and g == 1:
                     quantise("st", 1, 2)
                     quantise("s", 1, 2)
                 if i == 1:
@@ -346,53 +363,50 @@ def tile_brainquantumlayer_pc_t_kernel(tc, state, weights, J, theta, lam, mask, 
                         tanh_new_state(i - 1, 0, 256)
                     if ok(co):
                         stage2(co, 2, 1, "os")
-                        stage2(co, 0, 0, "ov")
+                        stage2(co, 3, 1, "ov")
                         out_scalar(co, 2, 1)
-                    if i > 0 and ok(i + 2):
-                        transpose_state(i + 2, 0)
-                        transpose_state(i + 2, 1)
-                        copy_state(i + 2, 0)
+                        out_scalar(co, 3, 1)
                     if i > 0:
                         transpose_noise(i, 1)
                 if g == 1:
                     if ok(i - 1):
                         tanh_new_state(i - 1, 256, 256)
                     if ok(co):
-                        out_vector(co, 0, 0)
-                        store(co, 0)
-                        stage2(co, 3, 1, "os")
+                        stage2(co, 0, 0, "os")
                         stage2(co, 1, 0, "ov")
-                        out_scalar(co, 3, 1)
+                        out_scalar(co, 0, 0)
                     if ok(i + 1):
                         transpose_noise(i + 1, 0)
                     if i == 0:
                         transpose_state(2, 0)
                         transpose_state(2, 1)
-                        copy_state(2, 0)
+                        tanh_state_f32(2, 0)
+                        round_s(2, 0)
+                        tanh_state_f32(2, 1)
+                        round_s(2, 1)
+                    if ok(i + 2):
+                        copy_state(i + 2, 0)
+                        copy_state(i + 2, 1)
                 if g == 2:
                     if ok(co):
                         out_vector(co, 1, 0)
                         store(co, 1)
-                        stage2(co, 3, 0, "os")
-                        stage2(co, 2, 0, "ov")
-                    if ok(i + 2):
-                        copy_state(i + 2, 1)
+                        store(co, 0)
+                        stage2(co, 2, 0, "os")
+                        stage2(co, 3, 0, "ov")
                 if g == 3:
                     if i == N_CHUNKS - 1:
                         quantise_new_state(i - 1, 0, CHUNK)
                         stage2(i - 1, 0, 1, "ts0")
                         stage2(i - 1, 1, 1, "ts1")
                     if ok(co):
-                        if i >= LATE:
-                            out_scalar(co, 2, 0)
-                        else:
-                            out_vector(co, 2, 0)
+                        out_vector(co, 2, 0)
                         store(co, 2)
                         out_vector(co, 3, 0)
                         store(co, 3)
-                    if ok(i + 2):
-                        tanh_state_bf16(i + 2, 0)
-                        tanh_state_bf16(i + 2, 1)
+                    if ok(i + 3):
+                        transpose_state(i + 3, 0)
+                        transpose_state(i + 3, 1)
 
         last = N_CHUNKS - 1
         out_scalar(last - 1, 0, 1)

import math
from contextlib import ExitStack

import concourse.mybir as mybir
from concourse.masks import make_identity

F32 = mybir.dt.float32
BF16 = mybir.dt.bfloat16
I32 = mybir.dt.int32
U32 = mybir.dt.uint32
U8 = mybir.dt.uint8
FP8X4 = mybir.dt.float8_e4m3fn_x4
ALU = mybir.AluOpType
ACT = mybir.ActivationFunctionType

P = 128
TOKENS = 4096
NEURONS = 512
OUTS = 1024
CHUNK = 512
N_CHUNKS = TOKENS // CHUNK
GROUPS = 4 * N_CHUNKS
LAG_OUT = 6
PI_HI = 3.1415927410125732
PI_LO = -8.742277657347586e-08
PINNED = True
W_OUT_ON_SCALAR = 2
LATE = 8

FLOPS = 2 * TOKENS * NEURONS * (2 * NEURONS + OUTS)


def tile_brainquantumlayer_pc_t_kernel(tc, state, weights, J, theta, lam, mask, noise_raw, W_out, b_out, out):
    nc = tc.nc
    with ExitStack() as ctx:
        if PINNED:
            ctx.enter_context(tc.manual_schedule())
        const = ctx.enter_context(tc.tile_pool(name="const", bufs=1))
        work = ctx.enter_context(tc.tile_pool(name="work", bufs=2))
        psum = ctx.enter_context(tc.psum_pool(name="psum", bufs=1))

        ident = const.tile([P, P], F32, name="ident")
        st_all = const.tile([P, N_CHUNKS * 2048], BF16, name="st_all")
        nz_all = const.tile([P, N_CHUNKS * 2048], BF16, name="nz_all")
        th_raw = const.tile([P, 4], BF16, name="th_raw")
        lam_raw = const.tile([P, 1], BF16, name="lam_raw")
        b_bc = const.tile([P, OUTS], BF16, name="b_bc")
        w_raw = const.tile([P, 2048], BF16, name="w_raw")
        m_raw = const.tile([P, 2048], BF16, name="m_raw")
        j_raw = const.tile([P, 2048], BF16, name="j_raw")
        wo_raw = const.tile([P, 4096], BF16, name="wo_raw")
        g_w = const.tile([P, 2048], BF16, name="g_w", align_bytes=64)
        g_j = const.tile([P, 2048], BF16, name="g_j", align_bytes=64)
        g_wo = const.tile([P, 4096], BF16, name="g_wo", align_bytes=64)
        c_w = const.tile([P, 512], U32, name="c_w", align_bytes=64)
        c_j = const.tile([P, 512], U32, name="c_j", align_bytes=64)
        c_wo = const.tile([P, 1024], U32, name="c_wo", align_bytes=64)
        s_w = const.tile([P, 512], U8, name="s_w", align_bytes=64)
        s_j = const.tile([P, 512], U8, name="s_j", align_bytes=64)
        s_wo = const.tile([P, 1024], U8, name="s_wo", align_bytes=64)
        lam_f = const.tile([P, 1], F32, name="lam_f")
        t01 = const.tile([P, 4], F32, name="t01")

        st_words = st_all[:].bitcast(F32)
        nz_words = nz_all[:].bitcast(F32)

        def load_rows(dst, src, c):
            nc.sync.dma_start(
                out=dst[:, c * 2048 : (c + 1) * 2048],
                in_=src[c * CHUNK : (c + 1) * CHUNK, :].rearrange("(p j) k -> p (j k)", j=4),
            )

        def load_k_first(dst, src):
            nc.sync.dma_start(
                out=dst[:].rearrange("p (u x) -> p u x", u=2),
                in_=src.rearrange("(u p e) n -> p u (e n)", u=2, e=2),
            )

        nc.scalar.dma_start(out=th_raw[:].rearrange("p (u e) -> p u e", u=2), in_=theta.rearrange("(u p e) -> p u e", u=2, e=2))
        nc.scalar.dma_start(out=lam_raw[:], in_=lam.partition_broadcast(P))
        make_identity(nc, ident[:])
        load_rows(st_all, state, 0)
        load_k_first(m_raw, mask)
        load_k_first(j_raw, J)
        load_k_first(w_raw, weights)
        load_rows(nz_all, noise_raw, 0)
        load_rows(st_all, state, 1)
        nc.sync.dma_start(out=wo_raw[:].rearrange("p (r k) -> p r k", r=8), in_=W_out.rearrange("(r p) k -> p r k", p=P))
        load_rows(nz_all, noise_raw, 1)
        load_rows(st_all, state, 2)
        nc.sync.dma_start(out=b_bc[:], in_=b_out.partition_broadcast(P))
        load_rows(nz_all, noise_raw, 2)
        for c in range(3, N_CHUNKS):
            load_rows(st_all, state, c)
            load_rows(nz_all, noise_raw, c)

        x2 = const.tile([P, 4], F32, name="x2")
        yy = const.tile([P, 4], F32, name="yy")
        ki = const.tile([P, 4], I32, name="ki")
        kf = const.tile([P, 4], F32, name="kf")
        r1 = const.tile([P, 4], F32, name="r1")
        r2 = const.tile([P, 4], F32, name="r2")
        sn = const.tile([P, 4], F32, name="sn")
        nc.vector.tensor_scalar(out=yy[:], in0=th_raw[:], scalar1=2.0 / math.pi, scalar2=None, op0=ALU.mult)
        nc.vector.tensor_scalar(out=x2[:], in0=th_raw[:], scalar1=2.0, scalar2=None, op0=ALU.mult)
        nc.vector.tensor_copy(out=ki[:], in_=yy[:])
        nc.vector.tensor_copy(out=kf[:], in_=ki[:])
        nc.vector.scalar_tensor_tensor(out=r1[:], in0=kf[:], scalar=-PI_HI, in1=x2[:], op0=ALU.mult, op1=ALU.add)
        nc.vector.scalar_tensor_tensor(out=r2[:], in0=kf[:], scalar=-PI_LO, in1=r1[:], op0=ALU.mult, op1=ALU.add)
        nc.scalar.activation(out=sn[:], in_=r2[:], func=ACT.Sin)
        nc.scalar.activation(out=t01[:], in_=sn[:], func=ACT.Abs, scale=0.1)
        nc.vector.tensor_copy(out=lam_f[:], in_=lam_raw[:])

        def masked_weights(eng, raw, grouped, u):
            eng.tensor_tensor(
                out=grouped[:, u * 1024 : (u + 1) * 1024].rearrange("p (e q t) -> p e q t", e=2, t=4),
                in0=raw[:].rearrange("p (t u q e) -> p u e q t", t=4, u=2, e=2)[:, u],
                in1=m_raw[:].rearrange("p (t u q e) -> p u e q t", t=4, u=2, e=2)[:, u],
                op=ALU.mult,
            )

        tiles = {}

        def transpose_state(c, h):
            ts = psum.tile([P, 512], F32, name="ts%d" % h)
            tiles[("ts", c, h)] = ts
            for jj in range(2):
                for u in range(2):
                    col = c * 1024 + (2 * h + jj) * 256 + u * 128
                    nc.tensor.transpose(out=ts[:, u * 256 + jj * 128 : u * 256 + (jj + 1) * 128], in_=st_words[:, col : col + 128], identity=ident[:])

        def copy_state(c, h):
            if h == 0:
                tiles[("gst", c)] = work.tile([P, 2048], BF16, name="gst", align_bytes=64)
            ts = tiles[("ts", c, h)]
            nc.scalar.copy(
                out=tiles[("gst", c)][:].bitcast(F32)[:, h * 512 : (h + 1) * 512].rearrange("p (m u) -> p m u", u=2),
                in_=ts[:].rearrange("p (u m) -> p m u", u=2),
            )

        def tanh_state_bf16(c, h):
            if h == 0:
                tiles[("gs", c)] = work.tile([P, 2048], BF16, name="gs", align_bytes=64)
            ts = tiles[("ts", c, h)]
            nc.scalar.activation(
                out=tiles[("gs", c)][:, h * 1024 : (h + 1) * 1024].rearrange("p (m u e) -> p m u e", u=2, e=2),
                in_=ts[:].bitcast(BF16).rearrange("p (u m e) -> p m u e", u=2, e=2),
                func=ACT.Tanh,
            )

        def tanh_state_f32(c, h):
            if h == 0:
                tiles[("sf", c)] = work.tile([P, 2048], F32, name="sf", bufs=3)
            ts = tiles[("ts", c, h)]
            nc.scalar.activation(
                out=tiles[("sf", c)][:].rearrange("p (u e x) -> p u e x", u=2, e=2)[:, :, :, h * 256 : (h + 1) * 256],
                in_=ts[:].bitcast(BF16).rearrange("p (u m e) -> p u e m", u=2, e=2),
                func=ACT.Tanh,
            )

        def round_s(c, h):
            if h == 0:
                tiles[("gs", c)] = work.tile([P, 2048], BF16, name="gs", align_bytes=64)
            nc.gpsimd.tensor_scalar(
                out=tiles[("gs", c)][:, h * 1024 : (h + 1) * 1024].rearrange("p (m t) -> p m t", t=4),
                in0=tiles[("sf", c)][:].rearrange("p (t m) -> p m t", t=4)[:, h * 256 : (h + 1) * 256, :],
                scalar1=1.0,
                scalar2=0.0,
                op0=ALU.mult,
                op1=ALU.add,
            )

        def quantise(key, c, bufs):
            codes = work.tile([P, 512], U32, name="c" + key, bufs=bufs, align_bytes=64)
            scales = work.tile([P, 512], U8, name="s" + key, bufs=bufs, align_bytes=64)
            tiles[("c" + key, c)] = codes
            tiles[("s" + key, c)] = scales
            nc.vector.quantize_mx(out=codes[:].bitcast(FP8X4), scales=scales[:], in_=tiles[("g" + key, c)][:])

        def transpose_noise(c, u):
            tn = psum.tile([P, 512], F32, name="tn%d" % u)
            tiles[("tn", c, u)] = tn
            for j in range(4):
                col = c * 1024 + j * 256 + u * 128
                nc.tensor.transpose(out=tn[:, j * 128 : (j + 1) * 128], in_=nz_words[:, col : col + 128], identity=ident[:])

        def stage1(kind, c, t):
            acc = psum.tile([P, 512], F32, name="p" + kind)
            tiles[("p" + kind, c, t)] = acc
            cw, sw, key = (c_j, s_j, "s") if kind == "d" else (c_w, s_w, "st")
            nc.tensor.matmul_mx(
                out=acc[:],
                lhsT=cw[:, t * P : (t + 1) * P].bitcast(FP8X4),
                lhsT_scale=sw[:, t * P : (t + 1) * P],
                rhs=tiles[("c" + key, c)][:].bitcast(FP8X4),
                rhs_scale=tiles[("s" + key, c)][:],
                start=True,
                stop=True,
            )

        def delta_times_s(c, t):
            d = work.tile([P, 512], F32, name="d")
            tiles[("d", c, t)] = d
            nc.vector.scalar_tensor_tensor(
                out=d[:], in0=tiles[("pd", c, t)][:], scalar=lam_f[:, 0:1], in1=tiles[("sf", c)][:, t * 512 : (t + 1) * 512], op0=ALU.mult, op1=ALU.mult
            )

        def add_noise(c, t):
            e = work.tile([P, 512], F32, name="e")
            tiles[("e", c, t)] = e
            nc.vector.scalar_tensor_tensor(
                out=e[:],
                in0=tiles[("tn", c, t // 2)][:].bitcast(BF16).rearrange("p (m e) -> p e m", e=2)[:, t % 2, :],
                scalar=t01[:, t : t + 1],
                in1=tiles[("d", c, t)][:],
                op0=ALU.mult,
                op1=ALU.add,
            )

        def add_signal(c, t):
            if t == 0:
                tiles[("f", c)] = work.tile([P, 2048], F32, name="f")
            nc.vector.tensor_tensor(out=tiles[("f", c)][:, t * 512 : (t + 1) * 512], in0=tiles[("ps", c, t)][:], in1=tiles[("e", c, t)][:], op=ALU.add)

        def tanh_new_state(c, lo, n):
            if lo == 0:
                tiles[("gns", c)] = work.tile([P, 2048], BF16, name="gns", align_bytes=64)
            nc.scalar.activation(
                out=tiles[("gns", c)][:, lo * 4 : (lo + n) * 4].rearrange("p (m t) -> p m t", t=4),
                in_=tiles[("f", c)][:].rearrange("p (t m) -> p m t", t=4)[:, lo : lo + n, :],
                func=ACT.Tanh,
            )

        def quantise_new_state(c, lo, n):
            if lo == 0:
                tiles[("cns", c)] = work.tile([P, 512], U32, name="cns", bufs=3, align_bytes=64)
                tiles[("sns", c)] = work.tile([P, 512], U8, name="sns", bufs=3, align_bytes=64)
            nc.vector.quantize_mx(
                out=tiles[("cns", c)][:, lo : lo + n].bitcast(FP8X4),
                scales=tiles[("sns", c)][:, lo : lo + n],
                in_=tiles[("gns", c)][:, lo * 4 : (lo + n) * 4],
            )

        def stage2(c, j, o, tag):
            acc = psum.tile([P, 512], F32, name=tag)
            tiles[("po", c, j, o)] = acc
            nc.tensor.matmul_mx(
                out=acc[:],
                lhsT=tiles[("cns", c)][:, j * P : (j + 1) * P].bitcast(FP8X4),
                lhsT_scale=tiles[("sns", c)][:, j * P : (j + 1) * P],
                rhs=c_wo[:, o * 512 : (o + 1) * 512].bitcast(FP8X4),
                rhs_scale=s_wo[:, o * 512 : (o + 1) * 512],
                start=True,
                stop=True,
            )

        def out_tile(c, j):
            if ("ot", c, j) not in tiles:
                tiles[("ot", c, j)] = work.tile([P, OUTS], F32, name="ot", bufs=6)
            return tiles[("ot", c, j)]

        def out_vector(c, j, o):
            cols = slice(o * 512, (o + 1) * 512)
            nc.vector.tensor_tensor(out=out_tile(c, j)[:, cols], in0=tiles[("po", c, j, o)][:], in1=b_bc[:, cols], op=ALU.add)

        def out_scalar(c, j, o):
            cols = slice(o * 512, (o + 1) * 512)
            ot = out_tile(c, j)
            nc.scalar.copy(out=ot[:, cols], in_=tiles[("po", c, j, o)][:])
            nc.gpsimd.tensor_tensor(out=ot[:, cols], in0=ot[:, cols], in1=b_bc[:, cols], op=ALU.add)

        def store(c, j):
            nc.sync.dma_start(out=out[c * CHUNK : (c + 1) * CHUNK, :].rearrange("(p j) o -> p j o", j=4)[:, j, :], in_=tiles[("ot", c, j)][:])

        def transpose_w_out(b):
            pw = psum.tile([P, 512], F32, name=("ov", "os")[b % 2])
            tiles[("pw", b)] = pw
            for rr in range(2):
                for u in range(2):
                    col = (2 * b + rr) * 256 + u * 128
                    nc.tensor.transpose(out=pw[:, u * 256 + rr * 128 : u * 256 + (rr + 1) * 128], in_=wo_raw[:].bitcast(F32)[:, col : col + 128], identity=ident[:])

        def copy_w_out(b):
            copier = nc.scalar.copy if b < W_OUT_ON_SCALAR else nc.vector.tensor_copy
            copier(
                out=g_wo[:].bitcast(F32)[:, b * 512 : (b + 1) * 512].rearrange("p (m u) -> p m u", u=2),
                in_=tiles[("pw", b)][:].rearrange("p (u m) -> p m u", u=2),
            )

        def ok(c):
            return 0 <= c < N_CHUNKS

        masked_weights(nc.vector, j_raw, g_j, 0)
        masked_weights(nc.vector, j_raw, g_j, 1)
        nc.vector.quantize_mx(out=c_j[:].bitcast(FP8X4), scales=s_j[:], in_=g_j[:])
        transpose_state(0, 0)
        transpose_state(0, 1)
        tanh_state_bf16(0, 0)
        tanh_state_bf16(0, 1)
        tanh_state_f32(0, 0)
        tanh_state_f32(0, 1)
        copy_state(0, 0)
        copy_state(0, 1)
        quantise("s", 0, 2)
        stage1("d", 0, 0)
        masked_weights(nc.vector, w_raw, g_w, 0)
        masked_weights(nc.vector, w_raw, g_w, 1)
        transpose_noise(0, 0)
        transpose_noise(0, 1)
        transpose_state(1, 0)
        transpose_state(1, 1)
        copy_state(1, 0)
        copy_state(1, 1)
        tanh_state_bf16(1, 0)
        tanh_state_bf16(1, 1)

        for i in range(N_CHUNKS):
            co = i - 2
            if i == 2:
                copy_w_out(3)
            if ok(co):
                quantise_new_state(co, 0, CHUNK)
            if i > 0 and ok(i + 1):
                quantise("st", i + 1, 2)
            if i == 2:
                nc.vector.quantize_mx(out=c_wo[:].bitcast(FP8X4), scales=s_wo[:], in_=g_wo[:])
            if i > 0 and ok(i + 1):
                quantise("s", i + 1, 2)
            if i == 0:
                tanh_state_f32(1, 0)
                tanh_state_f32(1, 1)
            if i > 0 and ok(i + 2):
                tanh_state_f32(i + 2, 0)
                round_s(i + 2, 0)
                tanh_state_f32(i + 2, 1)
                round_s(i + 2, 1)
            if ok(co):
                stage2(co, 0, 1, "os")
                stage2(co, 1, 1, "ov")
                out_scalar(co, 0, 1)
                out_scalar(co, 1, 1)
            for g in range(4):
                q = 4 * i + g
                delta_times_s(i, g)
                if ok((q + 1) // 4):
                    stage1("d", (q + 1) // 4, (q + 1) % 4)
                if q > 0:
                    add_signal((q - 1) // 4, (q - 1) % 4)
                else:
                    nc.vector.quantize_mx(out=c_w[:].bitcast(FP8X4), scales=s_w[:], in_=g_w[:])
                    quantise("st", 0, 2)
                stage1("s", i, g)
                add_noise(i, g)
                if i == 0 and g == 1:
                    quantise("st", 1, 2)
                    quantise("s", 1, 2)
                if i == 1:
                    if g > 0:
                        copy_w_out(g - 1)
                    transpose_w_out(g)
                if g == 0:
                    if ok(i - 1):
                        tanh_new_state(i - 1, 0, 256)
                    if ok(co):
                        stage2(co, 2, 1, "os")
                        stage2(co, 3, 1, "ov")
                        out_scalar(co, 2, 1)
                        out_scalar(co, 3, 1)
                    if i > 0:
                        transpose_noise(i, 1)
                if g == 1:
                    if ok(i - 1):
                        tanh_new_state(i - 1, 256, 256)
                    if ok(co):
                        stage2(co, 0, 0, "os")
                        stage2(co, 1, 0, "ov")
                        out_scalar(co, 0, 0)
                    if ok(i + 1):
                        transpose_noise(i + 1, 0)
                    if i == 0:
                        transpose_state(2, 0)
                        transpose_state(2, 1)
                        tanh_state_f32(2, 0)
                        round_s(2, 0)
                        tanh_state_f32(2, 1)
                        round_s(2, 1)
                    if ok(i + 2):
                        copy_state(i + 2, 0)
                        copy_state(i + 2, 1)
                if g == 2:
                    if ok(co):
                        out_vector(co, 1, 0)
                        store(co, 1)
                        store(co, 0)
                        stage2(co, 2, 0, "os")
                        stage2(co, 3, 0, "ov")
                if g == 3:
                    if i == N_CHUNKS - 1:
                        quantise_new_state(i - 1, 0, CHUNK)
                        stage2(i - 1, 0, 1, "ts0")
                        stage2(i - 1, 1, 1, "ts1")
                    if ok(co):
                        out_vector(co, 2, 0)
                        store(co, 2)
                        out_vector(co, 3, 0)
                        store(co, 3)
                    if ok(i + 3):
                        transpose_state(i + 3, 0)
                        transpose_state(i + 3, 1)

        last = N_CHUNKS - 1
        out_scalar(last - 1, 0, 1)
        out_scalar(last - 1, 1, 1)
        add_signal(last, 3)
        for j in range(4):
            tanh_new_state(last, j * P, P)
        for j, o, bank in ((0, 0, "ov"), (1, 0, "os"), (2, 0, "pd"), (2, 1, "ps"), (3, 0, "tn0"), (3, 1, "tn1")):
            stage2(last - 1, j, o, bank)
        out_vector(last - 1, 0, 0)
        store(last - 1, 0)
        out_vector(last - 1, 1, 0)
        store(last - 1, 1)
        out_vector(last - 1, 2, 0)
        out_vector(last - 1, 2, 1)
        store(last - 1, 2)
        quantise_new_state(last, 0, 256)
        out_vector(last - 1, 3, 0)
        out_vector(last - 1, 3, 1)
        store(last - 1, 3)
        quantise_new_state(last, 256, 256)
        for j, o, bank in ((0, 1, "ts0"), (0, 0, "ts1"), (1, 1, "ov"), (1, 0, "os"), (2, 0, "pd"), (2, 1, "ps"), (3, 0, "tn0"), (3, 1, "tn1")):
            stage2(last, j, o, bank)
        for j in range(4):
            if j < 2:
                out_scalar(last, j, 1)
            else:
                out_vector(last, j, 1)
            out_vector(last, j, 0)
            store(last, j)
